import numpy as np
import ml_dtypes


def mxq(x, axis, fmt="e4m3"):
    dtype, down = {"e4m3": (ml_dtypes.float8_e4m3fn, 7), "e5m2": (ml_dtypes.float8_e5m2, 14)}[fmt]
    v = np.moveaxis(np.asarray(x, np.float32).astype(ml_dtypes.bfloat16).astype(np.float64), axis, -1)
    blocks = v.reshape(v.shape[:-1] + (-1, 32))
    amax = np.abs(blocks).max(-1, keepdims=True)
    byte = np.maximum(np.where(amax > 0, np.frexp(amax)[1] - 1 + 127, 0) - down, 1)
    scale = np.exp2(byte - 127.0)
    codes = (blocks / scale).astype(np.float32).astype(dtype).astype(np.float64)
    return np.moveaxis((codes * scale).reshape(v.shape), -1, axis)


WIDE = False


def mx_kscale(k):
    if not WIDE:
        return np.ones(k)
    levels = np.array([10, -10, 5, -5, 0])
    a = np.random.permutation(np.resize(levels, k // 512 * 4)).reshape(k // 512, 4)
    idx = np.arange(k)
    return np.exp2(a[idx // 512, idx % 128 // 32])


BF16 = ml_dtypes.bfloat16


def bf(x):
    return np.asarray(x, np.float32).astype(BF16)


def f64(x):
    return np.asarray(x).astype(np.float64)


T, B, I, H = 32, 128, 512, 512


def sigmoid(v):
    return 1.0 / (1.0 + np.exp(-v))


def setup_inputs():
    s = mx_kscale(I)
    return {
        "input": bf(np.random.standard_normal((T, B, I)) * s),
        "h0": bf(np.random.standard_normal((B, H))),
        "c0": bf(np.random.standard_normal((B, H))),
        "noise": bf(np.random.standard_normal((B, H)) * 0.3),
        "W_ih": bf(np.random.standard_normal((4 * H, I)) / np.sqrt(I) / s[None, :]),
        "W_hh": bf(np.random.standard_normal((4 * H, H)) * 0.7 / np.sqrt(H)),
        "b_ih": bf(np.random.standard_normal(4 * H) * 0.3),
        "b_hh": bf(np.random.standard_normal(4 * H) * 0.3),
    }


def reference(input, h0, c0, noise, W_ih, W_hh, b_ih, b_hh):
    hsz = h0.shape[-1]
    gx = mxq(f64(input), 2, "e4m3") @ mxq(f64(W_ih), 1, "e4m3").T
    gh = f64(h0) @ f64(W_hh).T
    gates = gx + gh[None, :, :] + (f64(b_ih) + f64(b_hh))
    i_g = sigmoid(gates[..., 0 * hsz:1 * hsz])
    f_g = sigmoid(gates[..., 1 * hsz:2 * hsz])
    g_g = np.tanh(gates[..., 2 * hsz:3 * hsz])
    o_g = sigmoid(gates[..., 3 * hsz:4 * hsz])
    c = f_g * f64(c0)[None] + i_g * g_g
    h = o_g * np.tanh(c) + f64(noise)[None]
    return (h, np.stack([h[-1], c[-1]]))

@@ -1,0 +1,180 @@
+from contextlib import ExitStack
+
+import concourse.mybir as mybir
+from concourse.masks import make_identity
+
+F32 = mybir.dt.float32
+BF16 = mybir.dt.bfloat16
+U32 = mybir.dt.uint32
+U8 = mybir.dt.uint8
+FP8X4 = mybir.dt.float8_e4m3fn_x4
+ACT = mybir.ActivationFunctionType
+ALU = mybir.AluOpType
+
+T, B, I, H = 32, 128, 512, 512
+P = 128
+FLOPS = 2 * T * B * I * 4 * H + 2 * B * H * 4 * H
+
+GATE_ROW0 = (0, 512, 1536, 1024)
+U = 2
+QUAD = 4
+
+
+def tile_lstmlayer_kernel(tc, x_in, h0, c0, noise, w_ih, w_hh, b_ih, b_hh, out_h, out_state):
+    nc = tc.nc
+    with ExitStack() as ctx:
+        const = ctx.enter_context(tc.tile_pool(name="const", bufs=1))
+        raws = ctx.enter_context(tc.tile_pool(name="raws", bufs=16))
+        stage = ctx.enter_context(tc.tile_pool(name="stage", bufs=2))
+        work = ctx.enter_context(tc.tile_pool(name="work", bufs=3))
+        pconst = ctx.enter_context(tc.psum_pool(name="pconst", bufs=1))
+        pz = ctx.enter_context(tc.psum_pool(name="pz", bufs=4))
+        ptp = ctx.enter_context(tc.psum_pool(name="ptp", bufs=2))
+
+        ident_f = const.tile([P, P], F32, name="ident_f")
+        make_identity(nc, ident_f[:])
+        ident_b = const.tile([P, P], BF16, name="ident_b")
+        make_identity(nc, ident_b[:])
+        ones_b = const.tile([P, P], BF16, name="ones_b")
+        nc.vector.memset(ones_b[:], 1.0)
+        bias_rows = const.tile([P, 4 * H], BF16, name="bias_rows")
+        nc.vector.memset(bias_rows[:], 0.0)
+        warm = const.tile([P, 1], F32, name="warm")
+        nc.vector.memset(warm[:], 0.0)
+        warm2 = const.tile([P, 1], F32, name="warm2")
+        nc.scalar.activation(out=warm2[:], in_=warm[:], func=ACT.Sigmoid)
+
+        g_sb = const.tile([P, 4 * H], F32, name="g_sb")
+        w_codes = const.tile([P, 4 * H], U32, name="w_codes", align_bytes=64)
+        w_scales = const.tile([P, 4 * H], U8, name="w_scales", align_bytes=64)
+        x_codes = const.tile([P, T * B], U32, name="x_codes", align_bytes=64)
+        x_scales = const.tile([P, T * B], U8, name="x_scales", align_bytes=64)
+        whh_t = const.tile([P, 2, 4 * H], F32, name="whh_t")
+        h0_t = const.tile([P, 2, B], F32, name="h0_t")
+        h0_sb = const.tile([P, H], BF16, name="h0_sb")
+        c0_sb = const.tile([P, H], BF16, name="c0_sb")
+        noise_sb = const.tile([P, H], BF16, name="noise_sb")
+        whh_b = whh_t[:].bitcast(BF16).rearrange("w u (j e) -> w u j e", e=2)
+        h0_b = h0_t[:].bitcast(BF16).rearrange("w u (b e) -> w u b e", e=2)
+
+        def load_x(q):
+            raw = raws.tile([P, QUAD, I], BF16, tag="raw", name="xraw")
+            nc.sync.dma_start(out=raw[:], in_=x_in[QUAD * q:QUAD * (q + 1)].rearrange("t b k -> b t k"))
+            return raw
+
+        def load_w(w, cb):
+            r0 = GATE_ROW0[cb]
+            raw = raws.tile([P, 4, I], BF16, tag="raw", name="wraw")
+            nc.sync.dma_start(out=raw[:], in_=w[r0:r0 + 512, :].rearrange("(p a) k -> p a k", a=4))
+            return raw
+
+        x_raw = [load_x(0)]
+        wih_raw = [load_w(w_ih, 0)]
+        nc.sync.dma_start(out=h0_sb[:], in_=h0)
+        whh_raw = [load_w(w_hh, 0)]
+        nc.sync.dma_start(out=bias_rows[0:1, :], in_=b_ih.rearrange("(o n) -> o n", o=1))
+        nc.sync.dma_start(out=bias_rows[1:2, :], in_=b_hh.rearrange("(o n) -> o n", o=1))
+        nc.sync.dma_start(out=c0_sb[:], in_=c0)
+        for cb in range(1, 4):
+            wih_raw.append(load_w(w_ih, cb))
+            whh_raw.append(load_w(w_hh, cb))
+        nc.sync.dma_start(out=noise_sb[:], in_=noise)
+        for q in range(1, T // QUAD):
+            x_raw.append(load_x(q))
+
+        def prep_x(q):
+            rawf = x_raw[q][:].bitcast(F32)
+            grp = stage.tile([P, QUAD * B * 4], BF16, tag="xgrp", name="xgrp", align_bytes=64)
+            grpf = grp[:].bitcast(F32).rearrange("w (s b u) -> w s b u", s=QUAD, u=2)
+            for half in range(2):
+                pt = ptp.tile([P, 512], F32, tag="tp", name="pt")
+                for sl in range(2):
+                    for u in range(2):
+                        pl = 2 * sl + u
+                        nc.tensor.transpose(pt[:, pl * P:(pl + 1) * P], rawf[:, 2 * half + sl, u * P:(u + 1) * P], ident_f[:])
+                nc.scalar.copy(out=grpf[:, 2 * half:2 * half + 2, :, :],
+                               in_=pt[:].rearrange("w (s u b) -> w s b u", s=2, u=2))
+            cols = slice(q * QUAD * B, (q + 1) * QUAD * B)
+            nc.vector.quantize_mx(out=x_codes[:, cols].bitcast(FP8X4), scales=x_scales[:, cols], in_=grp[:])
+
+        def prep_wih(cb):
+            rawf = wih_raw[cb][:].bitcast(F32)
+            grp = stage.tile([P, 512 * 4], BF16, tag="wgrp", name="wgrp", align_bytes=64)
+            grpf = grp[:].bitcast(F32).rearrange("w (p a u) -> w p a u", a=4, u=2)
+            for half in range(2):
+                pt = pz.tile([P, 512], F32, tag="z", name="ptw")
+                for al in range(2):
+                    for u in range(2):
+                        pl = 2 * al + u
+                        nc.tensor.transpose(pt[:, pl * P:(pl + 1) * P], rawf[:, 2 * half + al, u * P:(u + 1) * P], ident_f[:])
+                nc.vector.tensor_copy(out=grpf[:, :, 2 * half:2 * half + 2, :],
+                                      in_=pt[:].rearrange("w (a u p) -> w p a u", a=2, u=2))
+            cols = slice(cb * 512, (cb + 1) * 512)
+            nc.vector.quantize_mx(out=w_codes[:, cols].bitcast(FP8X4), scales=w_scales[:, cols], in_=grp[:])
+
+        def prep_whh(cb):
+            rawf = whh_raw[cb][:].bitcast(F32)
+            for u in range(2):
+                pt = pz.tile([P, 512], F32, tag="z", name="pth")
+                for a in range(4):
+                    nc.tensor.transpose(pt[:, a * P:(a + 1) * P], rawf[:, a, u * P:(u + 1) * P], ident_f[:])
+                nc.scalar.copy(out=whh_t[:, u, cb * 512:(cb + 1) * 512].rearrange("w (p a) -> w p a", a=4),
+                               in_=pt[:].rearrange("w (a p) -> w p a", a=4))
+
+        def make_g(cb):
+            r0 = GATE_ROW0[cb]
+            cols = slice(cb * 512, (cb + 1) * 512)
+            zt = pz.tile([P, 512], F32, tag="z", name="zg")
+            for u in range(2):
+                for e in range(2):
+                    nc.tensor.matmul(zt[:], lhsT=h0_b[:, u, :, e], rhs=whh_b[:, u, cols, e],
+                                     start=(u == 0 and e == 0), stop=False)
+            nc.tensor.matmul(zt[:], lhsT=ones_b[:], rhs=bias_rows[:, r0:r0 + 512], start=False, stop=True)
+            nc.scalar.copy(out=g_sb[:, cols], in_=zt[:])
+
+        prep_x(0)
+        pth0 = ptp.tile([P, 512], F32, tag="tp", name="pth0")
+        h0f = h0_sb[:].bitcast(F32)
+        for u in range(2):
+            nc.tensor.transpose(pth0[:, u * P:(u + 1) * P], h0f[:, u * P:(u + 1) * P], ident_f[:])
+        nc.vector.tensor_copy(out=h0_t[:].rearrange("w u b -> w (u b)"), in_=pth0[:, 0:2 * P])
+        for cb in range(4):
+            prep_wih(cb)
+            prep_whh(cb)
+            make_g(cb)
+        c0_p = pconst.tile([P, H], F32, name="c0_p")
+        nc.tensor.matmul(c0_p[:], lhsT=ident_b[:], rhs=c0_sb[:], start=True, stop=True)
+        noise_p = pconst.tile([P, H], F32, name="noise_p")
+        nc.tensor.matmul(noise_p[:], lhsT=ident_b[:], rhs=noise_sb[:], start=True, stop=True)
+        c0_bc = c0_p[:].unsqueeze(1).to_broadcast([P, U, H])
+        noise_bc = noise_p[:].unsqueeze(1).to_broadcast([P, U, H])
+
+        units_per_quad = QUAD // U
+        for n in range(T // U):
+            if n % units_per_quad == 0 and n // units_per_quad + 1 < T // QUAD:
+                prep_x(n // units_per_quad + 1)
+            a = work.tile([P, U, 4 * H], F32, tag="a", name="a")
+            for s in range(U):
+                t = n * U + s
+                xc = slice(t * B, (t + 1) * B)
+                for cb in range(4):
+                    cols = slice(cb * 512, (cb + 1) * 512)
+                    z = pz.tile([P, 512], F32, tag="z", name="z")
+                    nc.tensor.matmul_mx(z[:], lhsT=x_codes[:, xc].bitcast(FP8X4), lhsT_scale=x_scales[:, xc],
+                                        rhs=w_codes[:, cols].bitcast(FP8X4), rhs_scale=w_scales[:, cols],
+                                        start=True, stop=True)
+                    nc.vector.tensor_tensor(out=a[:, s, cols], in0=z[:], in1=g_sb[:, cols], op=ALU.add)
+            nc.scalar.activation(out=a[:, :, 0:1536], in_=a[:, :, 0:1536], func=ACT.Sigmoid)
+            nc.scalar.activation(out=a[:, :, 1536:2048], in_=a[:, :, 1536:2048], func=ACT.Tanh)
+            cst = work.tile([P, U, H], F32, tag="cst", name="cst")
+            nc.vector.tensor_tensor(out=cst[:], in0=a[:, :, 512:1024], in1=c0_bc, op=ALU.mult)
+            nc.gpsimd.tensor_tensor(out=a[:, :, 0:512], in0=a[:, :, 0:512], in1=a[:, :, 1536:2048], op=ALU.mult)
+            nc.gpsimd.tensor_tensor(out=cst[:], in0=cst[:], in1=a[:, :, 0:512], op=ALU.add)
+            hh = work.tile([P, U, H], F32, tag="hh", name="hh")
+            nc.scalar.activation(out=hh[:], in_=cst[:], func=ACT.Tanh)
+            nc.gpsimd.tensor_tensor(out=hh[:], in0=hh[:], in1=a[:, :, 1024:1536], op=ALU.mult)
+            nc.vector.tensor_tensor(out=hh[:], in0=hh[:], in1=noise_bc, op=ALU.add)
+            nc.sync.dma_start(out=out_h[n * U:(n + 1) * U].rearrange("t b h -> b t h"), in_=hh[:])
+            if n == T // U - 1:
+                nc.sync.dma_start(out=out_state[0], in_=hh[:, U - 1, :])
+                nc.sync.dma_start(out=out_state[1], in_=cst[:, U - 1, :])

@@ -15,21 +15,27 @@ T, B, I, H = 32, 128, 512, 512
 P = 128
 FLOPS = 2 * T * B * I * 4 * H + 2 * B * H * 4 * H
 
-GATE_ROW0 = (0, 512, 1536, 1024)
+GI, GG, GF, GO = 0, 1, 2, 3
+GATE_ROW0 = (0, 1024, 512, 1536)
+GATE_FUNC = (ACT.Sigmoid, ACT.Tanh, ACT.Sigmoid, ACT.Sigmoid)
 U = 2
+K = T // U
 QUAD = 4
+NQ = T // QUAD
+A_BUFS = (4, 3, 3, 4)
 
 
 def tile_lstmlayer_kernel(tc, x_in, h0, c0, noise, w_ih, w_hh, b_ih, b_hh, out_h, out_state):
     nc = tc.nc
     with ExitStack() as ctx:
         const = ctx.enter_context(tc.tile_pool(name="const", bufs=1))
-        raws = ctx.enter_context(tc.tile_pool(name="raws", bufs=16))
+        raws = ctx.enter_context(tc.tile_pool(name="raws", bufs=12))
         stage = ctx.enter_context(tc.tile_pool(name="stage", bufs=2))
         work = ctx.enter_context(tc.tile_pool(name="work", bufs=3))
         pconst = ctx.enter_context(tc.psum_pool(name="pconst", bufs=1))
         pz = ctx.enter_context(tc.psum_pool(name="pz", bufs=4))
         ptp = ctx.enter_context(tc.psum_pool(name="ptp", bufs=2))
+        ctx.enter_context(tc.manual_schedule())
 
         ident_f = const.tile([P, P], F32, name="ident_f")
         make_identity(nc, ident_f[:])
@@ -68,23 +74,28 @@ def tile_lstmlayer_kernel(tc, x_in, h0, c0, noise, w_ih, w_hh, b_ih, b_hh, out_h
             nc.sync.dma_start(out=raw[:], in_=w[r0:r0 + 512, :].rearrange("(p a) k -> p a k", a=4))
             return raw
 
-        x_raw = [load_x(0)]
-        wih_raw = [load_w(w_ih, 0)]
         nc.sync.dma_start(out=h0_sb[:], in_=h0)
         whh_raw = [load_w(w_hh, 0)]
+        x_raw = [load_x(0)]
+        wih_raw = [load_w(w_ih, 0)]
         nc.sync.dma_start(out=bias_rows[0:1, :], in_=b_ih.rearrange("(o n) -> o n", o=1))
         nc.sync.dma_start(out=bias_rows[1:2, :], in_=b_hh.rearrange("(o n) -> o n", o=1))
-        nc.sync.dma_start(out=c0_sb[:], in_=c0)
         for cb in range(1, 4):
-            wih_raw.append(load_w(w_ih, cb))
             whh_raw.append(load_w(w_hh, cb))
+            wih_raw.append(load_w(w_ih, cb))
+            if cb == 1:
+                nc.sync.dma_start(out=c0_sb[:], in_=c0)
         nc.sync.dma_start(out=noise_sb[:], in_=noise)
-        for q in range(1, T // QUAD):
+        for q in range(1, NQ):
             x_raw.append(load_x(q))
 
-        def prep_x(q):
+        x_grp = {}
+        w_grp = {}
+
+        def x_transpose(q):
             rawf = x_raw[q][:].bitcast(F32)
             grp = stage.tile([P, QUAD * B * 4], BF16, tag="xgrp", name="xgrp", align_bytes=64)
+            x_grp[q] = grp
             grpf = grp[:].bitcast(F32).rearrange("w (s b u) -> w s b u", s=QUAD, u=2)
             for half in range(2):
                 pt = ptp.tile([P, 512], F32, tag="tp", name="pt")
@@ -94,12 +105,22 @@ def tile_lstmlayer_kernel(tc, x_in, h0, c0, noise, w_ih, w_hh, b_ih, b_hh, out_h
                         nc.tensor.transpose(pt[:, pl * P:(pl + 1) * P], rawf[:, 2 * half + sl, u * P:(u + 1) * P], ident_f[:])
                 nc.scalar.copy(out=grpf[:, 2 * half:2 * half + 2, :, :],
                                in_=pt[:].rearrange("w (s u b) -> w s b u", s=2, u=2))
-            cols = slice(q * QUAD * B, (q + 1) * QUAD * B)
-            nc.vector.quantize_mx(out=x_codes[:, cols].bitcast(FP8X4), scales=x_scales[:, cols], in_=grp[:])
 
-        def prep_wih(cb):
+        def x_quantise(q):
+            cols = slice(q * QUAD * B, (q + 1) * QUAD * B)
+            nc.vector.quantize_mx(out=x_codes[:, cols].bitcast(FP8X4), scales=x_scales[:, cols], in_=x_grp[q][:])
+
+        def h0_transpose():
+            pt = ptp.tile([P, 512], F32, tag="tp", name="pth0")
+            h0f = h0_sb[:].bitcast(F32)
+            for u in range(2):
+                nc.tensor.transpose(pt[:, u * P:(u + 1) * P], h0f[:, u * P:(u + 1) * P], ident_f[:])
+            nc.vector.tensor_copy(out=h0_t[:].rearrange("w u b -> w (u b)"), in_=pt[:, 0:2 * P])
+
+        def wih_transpose(cb):
             rawf = wih_raw[cb][:].bitcast(F32)
             grp = stage.tile([P, 512 * 4], BF16, tag="wgrp", name="wgrp", align_bytes=64)
+            w_grp[cb] = grp
             grpf = grp[:].bitcast(F32).rearrange("w (p a u) -> w p a u", a=4, u=2)
             for half in range(2):
                 pt = pz.tile([P, 512], F32, tag="z", name="ptw")
@@ -109,10 +130,12 @@ def tile_lstmlayer_kernel(tc, x_in, h0, c0, noise, w_ih, w_hh, b_ih, b_hh, out_h
                         nc.tensor.transpose(pt[:, pl * P:(pl + 1) * P], rawf[:, 2 * half + al, u * P:(u + 1) * P], ident_f[:])
                 nc.vector.tensor_copy(out=grpf[:, :, 2 * half:2 * half + 2, :],
                                       in_=pt[:].rearrange("w (a u p) -> w p a u", a=2, u=2))
-            cols = slice(cb * 512, (cb + 1) * 512)
-            nc.vector.quantize_mx(out=w_codes[:, cols].bitcast(FP8X4), scales=w_scales[:, cols], in_=grp[:])
 
-        def prep_whh(cb):
+        def wih_quantise(cb):
+            cols = slice(cb * 512, (cb + 1) * 512)
+            nc.vector.quantize_mx(out=w_codes[:, cols].bitcast(FP8X4), scales=w_scales[:, cols], in_=w_grp[cb][:])
+
+        def whh_transpose(cb):
             rawf = whh_raw[cb][:].bitcast(F32)
             for u in range(2):
                 pt = pz.tile([P, 512], F32, tag="z", name="pth")
@@ -125,56 +148,113 @@ def tile_lstmlayer_kernel(tc, x_in, h0, c0, noise, w_ih, w_hh, b_ih, b_hh, out_h
             r0 = GATE_ROW0[cb]
             cols = slice(cb * 512, (cb + 1) * 512)
             zt = pz.tile([P, 512], F32, tag="z", name="zg")
+            nc.tensor.matmul(zt[:], lhsT=ones_b[:], rhs=bias_rows[:, r0:r0 + 512], start=True, stop=False)
             for u in range(2):
                 for e in range(2):
                     nc.tensor.matmul(zt[:], lhsT=h0_b[:, u, :, e], rhs=whh_b[:, u, cols, e],
-                                     start=(u == 0 and e == 0), stop=False)
-            nc.tensor.matmul(zt[:], lhsT=ones_b[:], rhs=bias_rows[:, r0:r0 + 512], start=False, stop=True)
+                                     start=False, stop=(u == 1 and e == 1))
             nc.scalar.copy(out=g_sb[:, cols], in_=zt[:])
 
-        prep_x(0)
-        pth0 = ptp.tile([P, 512], F32, tag="tp", name="pth0")
-        h0f = h0_sb[:].bitcast(F32)
-        for u in range(2):
-            nc.tensor.transpose(pth0[:, u * P:(u + 1) * P], h0f[:, u * P:(u + 1) * P], ident_f[:])
-        nc.vector.tensor_copy(out=h0_t[:].rearrange("w u b -> w (u b)"), in_=pth0[:, 0:2 * P])
-        for cb in range(4):
-            prep_wih(cb)
-            prep_whh(cb)
-            make_g(cb)
         c0_p = pconst.tile([P, H], F32, name="c0_p")
-        nc.tensor.matmul(c0_p[:], lhsT=ident_b[:], rhs=c0_sb[:], start=True, stop=True)
         noise_p = pconst.tile([P, H], F32, name="noise_p")
-        nc.tensor.matmul(noise_p[:], lhsT=ident_b[:], rhs=noise_sb[:], start=True, stop=True)
         c0_bc = c0_p[:].unsqueeze(1).to_broadcast([P, U, H])
         noise_bc = noise_p[:].unsqueeze(1).to_broadcast([P, U, H])
 
-        units_per_quad = QUAD // U
-        for n in range(T // U):
-            if n % units_per_quad == 0 and n // units_per_quad + 1 < T // QUAD:
-                prep_x(n // units_per_quad + 1)
-            a = work.tile([P, U, 4 * H], F32, tag="a", name="a")
+        a_t = {}
+        c_t = {}
+        h_t = {}
+
+        def gate(k, cb):
+            a = work.tile([P, U, H], F32, tag="a%d" % cb, name="a%d" % cb, bufs=A_BUFS[cb])
+            a_t[(k, cb)] = a
+            cols = slice(cb * 512, (cb + 1) * 512)
             for s in range(U):
-                t = n * U + s
+                t = k * U + s
                 xc = slice(t * B, (t + 1) * B)
-                for cb in range(4):
-                    cols = slice(cb * 512, (cb + 1) * 512)
-                    z = pz.tile([P, 512], F32, tag="z", name="z")
-                    nc.tensor.matmul_mx(z[:], lhsT=x_codes[:, xc].bitcast(FP8X4), lhsT_scale=x_scales[:, xc],
-                                        rhs=w_codes[:, cols].bitcast(FP8X4), rhs_scale=w_scales[:, cols],
-                                        start=True, stop=True)
-                    nc.vector.tensor_tensor(out=a[:, s, cols], in0=z[:], in1=g_sb[:, cols], op=ALU.add)
-            nc.scalar.activation(out=a[:, :, 0:1536], in_=a[:, :, 0:1536], func=ACT.Sigmoid)
-            nc.scalar.activation(out=a[:, :, 1536:2048], in_=a[:, :, 1536:2048], func=ACT.Tanh)
-            cst = work.tile([P, U, H], F32, tag="cst", name="cst")
-            nc.vector.tensor_tensor(out=cst[:], in0=a[:, :, 512:1024], in1=c0_bc, op=ALU.mult)
-            nc.gpsimd.tensor_tensor(out=a[:, :, 0:512], in0=a[:, :, 0:512], in1=a[:, :, 1536:2048], op=ALU.mult)
-            nc.gpsimd.tensor_tensor(out=cst[:], in0=cst[:], in1=a[:, :, 0:512], op=ALU.add)
-            hh = work.tile([P, U, H], F32, tag="hh", name="hh")
-            nc.scalar.activation(out=hh[:], in_=cst[:], func=ACT.Tanh)
-            nc.gpsimd.tensor_tensor(out=hh[:], in0=hh[:], in1=a[:, :, 1024:1536], op=ALU.mult)
+                z = pz.tile([P, 512], F32, tag="z", name="z")
+                nc.tensor.matmul_mx(z[:], lhsT=x_codes[:, xc].bitcast(FP8X4), lhsT_scale=x_scales[:, xc],
+                                    rhs=w_codes[:, cols].bitcast(FP8X4), rhs_scale=w_scales[:, cols],
+                                    start=True, stop=True)
+                nc.vector.tensor_tensor(out=a[:, s, :], in0=z[:], in1=g_sb[:, cols], op=ALU.add)
+            nc.scalar.activation(out=a[:], in_=a[:], func=GATE_FUNC[cb])
+
+        def st_a(k):
+            c = work.tile([P, U, H], F32, tag="c", name="c", bufs=3)
+            c_t[k] = c
+            nc.vector.tensor_tensor(out=c[:], in0=a_t[(k, GF)][:], in1=c0_bc, op=ALU.mult)
+
+        def st_b(k):
+            ai = a_t[(k, GI)]
+            nc.gpsimd.tensor_tensor(out=ai[:], in0=ai[:], in1=a_t[(k, GG)][:], op=ALU.mult)
+
+        def st_c(k):
+            eng = nc.vector if k == K - 1 else nc.gpsimd
+            eng.tensor_tensor(out=c_t[k][:], in0=c_t[k][:], in1=a_t[(k, GI)][:], op=ALU.add)
+
+        def st_tc(k):
+            hh = work.tile([P, U, H], F32, tag="hh", name="hh", bufs=4)
+            h_t[k] = hh
+            nc.scalar.activation(out=hh[:], in_=c_t[k][:], func=ACT.Tanh)
+
+        def st_x(k):
+            eng = nc.vector if k >= K - 2 else nc.gpsimd
+            eng.tensor_tensor(out=h_t[k][:], in0=h_t[k][:], in1=a_t[(k, GO)][:], op=ALU.mult)
+
+        def st_h(k):
+            hh = h_t[k]
             nc.vector.tensor_tensor(out=hh[:], in0=hh[:], in1=noise_bc, op=ALU.add)
-            nc.sync.dma_start(out=out_h[n * U:(n + 1) * U].rearrange("t b h -> b t h"), in_=hh[:])
-            if n == T // U - 1:
+            nc.sync.dma_start(out=out_h[k * U:(k + 1) * U].rearrange("t b h -> b t h"), in_=hh[:])
+            if k == K - 1:
                 nc.sync.dma_start(out=out_state[0], in_=hh[:, U - 1, :])
-                nc.sync.dma_start(out=out_state[1], in_=cst[:, U - 1, :])
+                nc.sync.dma_start(out=out_state[1], in_=c_t[k][:, U - 1, :])
+
+        h0_transpose()
+        whh_transpose(0)
+        x_transpose(0)
+        wih_transpose(0)
+        x_quantise(0)
+        make_g(0)
+        wih_quantise(0)
+        whh_transpose(1)
+        wih_transpose(1)
+
+        n_t = 1
+        n_q = 1
+        for it in range(K + 2):
+            if 0 <= it - 2 < K:
+                st_x(it - 2)
+            if 0 <= it - 1 < K:
+                st_a(it - 1)
+                st_c(it - 1)
+            if it < K:
+                gate(it, 0)
+                if it == 0:
+                    make_g(1)
+                    wih_quantise(1)
+                    whh_transpose(2)
+                    wih_transpose(2)
+                gate(it, 1)
+                st_b(it)
+                if it == 0:
+                    make_g(2)
+                    wih_quantise(2)
+                    nc.tensor.matmul(c0_p[:], lhsT=ident_b[:], rhs=c0_sb[:], start=True, stop=True)
+                    whh_transpose(3)
+                    wih_transpose(3)
+                gate(it, 2)
+            if 0 <= it - 1 < K:
+                st_tc(it - 1)
+            if it < K:
+                if it == 0:
+                    make_g(3)
+                    wih_quantise(3)
+                    nc.tensor.matmul(noise_p[:], lhsT=ident_b[:], rhs=noise_sb[:], start=True, stop=True)
+                gate(it, 3)
+            if 0 <= it - 2 < K:
+                st_h(it - 2)
+            if n_q < n_t:
+                x_quantise(n_q)
+                n_q += 1
+            if n_t < NQ and it < K and (min(it + 3, K - 1) * U + U - 1) // QUAD >= n_t:
+                x_transpose(n_t)
+                n_t += 1

@@ -22,7 +22,8 @@ U = 2
 K = T // U
 QUAD = 4
 NQ = T // QUAD
-A_BUFS = (4, 3, 3, 4)
+JT = H // P
+A_BUFS = (4, 3, 3, 5)
 
 
 def tile_lstmlayer_kernel(tc, x_in, h0, c0, noise, w_ih, w_hh, b_ih, b_hh, out_h, out_state):
@@ -34,7 +35,8 @@ def tile_lstmlayer_kernel(tc, x_in, h0, c0, noise, w_ih, w_hh, b_ih, b_hh, out_h
         work = ctx.enter_context(tc.tile_pool(name="work", bufs=3))
         pconst = ctx.enter_context(tc.psum_pool(name="pconst", bufs=1))
         pz = ctx.enter_context(tc.psum_pool(name="pz", bufs=4))
-        ptp = ctx.enter_context(tc.psum_pool(name="ptp", bufs=2))
+        pc = ctx.enter_context(tc.psum_pool(name="pc", bufs=2))
+        ptp = ctx.enter_context(tc.psum_pool(name="ptp", bufs=1))
         ctx.enter_context(tc.manual_schedule())
 
         ident_f = const.tile([P, P], F32, name="ident_f")
@@ -50,7 +52,8 @@ def tile_lstmlayer_kernel(tc, x_in, h0, c0, noise, w_ih, w_hh, b_ih, b_hh, out_h
         warm2 = const.tile([P, 1], F32, name="warm2")
         nc.scalar.activation(out=warm2[:], in_=warm[:], func=ACT.Sigmoid)
 
-        g_sb = const.tile([P, 4 * H], F32, name="g_sb")
+        g_t = const.tile([P, 3, JT, B], F32, name="g_t")
+        g_o = const.tile([P, H], F32, name="g_o")
         w_codes = const.tile([P, 4 * H], U32, name="w_codes", align_bytes=64)
         w_scales = const.tile([P, 4 * H], U8, name="w_scales", align_bytes=64)
         x_codes = const.tile([P, T * B], U32, name="x_codes", align_bytes=64)
@@ -60,6 +63,8 @@ def tile_lstmlayer_kernel(tc, x_in, h0, c0, noise, w_ih, w_hh, b_ih, b_hh, out_h
         h0_sb = const.tile([P, H], BF16, name="h0_sb")
         c0_sb = const.tile([P, H], BF16, name="c0_sb")
         noise_sb = const.tile([P, H], BF16, name="noise_sb")
+        c0t_sb = const.tile([P, JT, B], F32, name="c0t_sb")
+        c_last = const.tile([P, H], F32, name="c_last")
         whh_b = whh_t[:].bitcast(BF16).rearrange("w u (j e) -> w u j e", e=2)
         h0_b = h0_t[:].bitcast(BF16).rearrange("w u (b e) -> w u b e", e=2)
 
@@ -85,30 +90,29 @@ def tile_lstmlayer_kernel(tc, x_in, h0, c0, noise, w_ih, w_hh, b_ih, b_hh, out_h
             wih_raw.append(load_w(w_ih, cb))
             if cb == 1:
                 nc.sync.dma_start(out=c0_sb[:], in_=c0)
-        nc.sync.dma_start(out=noise_sb[:], in_=noise)
+                nc.sync.dma_start(out=noise_sb[:], in_=noise)
         for q in range(1, NQ):
             x_raw.append(load_x(q))
 
         x_grp = {}
         w_grp = {}
 
-        def x_transpose(q):
-            rawf = x_raw[q][:].bitcast(F32)
-            grp = stage.tile([P, QUAD * B * 4], BF16, tag="xgrp", name="xgrp", align_bytes=64)
-            x_grp[q] = grp
-            grpf = grp[:].bitcast(F32).rearrange("w (s b u) -> w s b u", s=QUAD, u=2)
-            for half in range(2):
-                pt = ptp.tile([P, 512], F32, tag="tp", name="pt")
-                for sl in range(2):
-                    for u in range(2):
-                        pl = 2 * sl + u
-                        nc.tensor.transpose(pt[:, pl * P:(pl + 1) * P], rawf[:, 2 * half + sl, u * P:(u + 1) * P], ident_f[:])
-                nc.scalar.copy(out=grpf[:, 2 * half:2 * half + 2, :, :],
-                               in_=pt[:].rearrange("w (s u b) -> w s b u", s=2, u=2))
+        def x_transpose(m):
+            rawf = x_raw[m * U // QUAD][:].bitcast(F32)
+            s0 = m * U % QUAD
+            grp = stage.tile([P, U * B * 4], BF16, tag="xgrp", name="xgrp", align_bytes=64)
+            x_grp[m] = grp
+            pt = ptp.tile([P, 512], F32, tag="tp", name="pt")
+            for sl in range(U):
+                for u in range(2):
+                    pl = 2 * sl + u
+                    nc.tensor.transpose(pt[:, pl * P:(pl + 1) * P], rawf[:, s0 + sl, u * P:(u + 1) * P], ident_f[:])
+            nc.scalar.copy(out=grp[:].bitcast(F32).rearrange("w (s b u) -> w s b u", s=U, u=2),
+                           in_=pt[:].rearrange("w (s u b) -> w s b u", s=U, u=2))
 
-        def x_quantise(q):
-            cols = slice(q * QUAD * B, (q + 1) * QUAD * B)
-            nc.vector.quantize_mx(out=x_codes[:, cols].bitcast(FP8X4), scales=x_scales[:, cols], in_=x_grp[q][:])
+        def x_quantise(m):
+            cols = slice(m * U * B, (m + 1) * U * B)
+            nc.vector.quantize_mx(out=x_codes[:, cols].bitcast(FP8X4), scales=x_scales[:, cols], in_=x_grp[m][:])
 
         def h0_transpose():
             pt = ptp.tile([P, 512], F32, tag="tp", name="pth0")
@@ -146,55 +150,114 @@ def tile_lstmlayer_kernel(tc, x_in, h0, c0, noise, w_ih, w_hh, b_ih, b_hh, out_h
 
         def make_g(cb):
             r0 = GATE_ROW0[cb]
-            cols = slice(cb * 512, (cb + 1) * 512)
             zt = pz.tile([P, 512], F32, tag="z", name="zg")
-            nc.tensor.matmul(zt[:], lhsT=ones_b[:], rhs=bias_rows[:, r0:r0 + 512], start=True, stop=False)
-            for u in range(2):
-                for e in range(2):
-                    nc.tensor.matmul(zt[:], lhsT=h0_b[:, u, :, e], rhs=whh_b[:, u, cols, e],
-                                     start=False, stop=(u == 1 and e == 1))
-            nc.scalar.copy(out=g_sb[:, cols], in_=zt[:])
+            if cb == GO:
+                cols = slice(cb * 512, (cb + 1) * 512)
+                nc.tensor.matmul(zt[:], lhsT=ones_b[:], rhs=bias_rows[:, r0:r0 + 512], start=True, stop=False)
+                for u in range(2):
+                    for e in range(2):
+                        nc.tensor.matmul(zt[:], lhsT=h0_b[:, u, :, e], rhs=whh_b[:, u, cols, e],
+                                         start=False, stop=(u == 1 and e == 1))
+                nc.scalar.copy(out=g_o[:], in_=zt[:])
+            else:
+                for jt in range(JT):
+                    js = slice(jt * P, (jt + 1) * P)
+                    nc.tensor.matmul(zt[:, js], lhsT=bias_rows[:, r0 + jt * P:r0 + (jt + 1) * P], rhs=ones_b[:],
+                                     start=True, stop=False)
+                    for u in range(2):
+                        for e in range(2):
+                            nc.tensor.matmul(zt[:, js], lhsT=whh_b[:, u, cb * 512 + jt * P:cb * 512 + (jt + 1) * P, e],
+                                             rhs=h0_b[:, u, :, e], start=False, stop=(u == 1 and e == 1))
+                nc.scalar.copy(out=g_t[:, cb, :, :].rearrange("p j b -> p (j b)"), in_=zt[:])
 
-        c0_p = pconst.tile([P, H], F32, name="c0_p")
-        noise_p = pconst.tile([P, H], F32, name="noise_p")
-        c0_bc = c0_p[:].unsqueeze(1).to_broadcast([P, U, H])
-        noise_bc = noise_p[:].unsqueeze(1).to_broadcast([P, U, H])
+        cn_p = pconst.tile([P, 2, H], BF16, name="cn_p")
+
+        def make_c0t():
+            for jt in range(JT):
+                js = slice(jt * P, (jt + 1) * P)
+                nc.tensor.matmul(cn_p[:, 0, js], lhsT=c0_sb[:, js], rhs=ident_b[:], start=True, stop=True)
+            nc.vector.tensor_copy(out=c0t_sb[:].rearrange("p j b -> p (j b)"), in_=cn_p[:, 0, :])
+
+        def make_noise():
+            nc.tensor.matmul(cn_p[:, 1, :], lhsT=ident_b[:], rhs=noise_sb[:], start=True, stop=True)
+
+        c0t_p = cn_p[:, 0, :].rearrange("p (j b) -> p j b", j=JT)
+        noise_bc = cn_p[:, 1, :].unsqueeze(1).to_broadcast([P, U, H])
 
         a_t = {}
         c_t = {}
+        cp_t = {}
         h_t = {}
 
-        def gate(k, cb):
-            a = work.tile([P, U, H], F32, tag="a%d" % cb, name="a%d" % cb, bufs=A_BUFS[cb])
+        def gate_mx(k, cb):
+            xc = slice(k * U * B, (k + 1) * U * B)
+            if cb == GO:
+                a = work.tile([P, U, H], F32, tag="a3", name="a3", bufs=A_BUFS[cb])
+                cols = slice(cb * 512, (cb + 1) * 512)
+                for s in range(U):
+                    t = k * U + s
+                    xs = slice(t * B, (t + 1) * B)
+                    z = pz.tile([P, 512], F32, tag="z", name="z")
+                    nc.tensor.matmul_mx(z[:], lhsT=x_codes[:, xs].bitcast(FP8X4), lhsT_scale=x_scales[:, xs],
+                                        rhs=w_codes[:, cols].bitcast(FP8X4), rhs_scale=w_scales[:, cols],
+                                        start=True, stop=True)
+                    nc.vector.tensor_tensor(out=a[:, s, :], in0=z[:], in1=g_o[:], op=ALU.add)
+            else:
+                a = work.tile([P, JT, U, B], F32, tag="a%d" % cb, name="a%d" % cb, bufs=A_BUFS[cb])
+                for bk in range(2):
+                    z = pz.tile([P, 512], F32, tag="z", name="z")
+                    for jl in range(2):
+                        jt = 2 * bk + jl
+                        wc = slice(cb * 512 + jt * P, cb * 512 + (jt + 1) * P)
+                        nc.tensor.matmul_mx(z[:, jl * U * B:(jl + 1) * U * B],
+                                            lhsT=w_codes[:, wc].bitcast(FP8X4), lhsT_scale=w_scales[:, wc],
+                                            rhs=x_codes[:, xc].bitcast(FP8X4), rhs_scale=x_scales[:, xc],
+                                            start=True, stop=True)
+                    nc.vector.tensor_tensor(out=a[:, 2 * bk:2 * bk + 2, :, :],
+                                            in0=z[:].rearrange("p (j t b) -> p j t b", j=2, t=U),
+                                            in1=g_t[:, cb, 2 * bk:2 * bk + 2, :].unsqueeze(2).to_broadcast([P, 2, U, B]),
+                                            op=ALU.add)
             a_t[(k, cb)] = a
-            cols = slice(cb * 512, (cb + 1) * 512)
-            for s in range(U):
-                t = k * U + s
-                xc = slice(t * B, (t + 1) * B)
-                z = pz.tile([P, 512], F32, tag="z", name="z")
-                nc.tensor.matmul_mx(z[:], lhsT=x_codes[:, xc].bitcast(FP8X4), lhsT_scale=x_scales[:, xc],
-                                    rhs=w_codes[:, cols].bitcast(FP8X4), rhs_scale=w_scales[:, cols],
-                                    start=True, stop=True)
-                nc.vector.tensor_tensor(out=a[:, s, :], in0=z[:], in1=g_sb[:, cols], op=ALU.add)
+
+        def gate_act(k, cb):
+            a = a_t[(k, cb)]
             nc.scalar.activation(out=a[:], in_=a[:], func=GATE_FUNC[cb])
 
         def st_a(k):
-            c = work.tile([P, U, H], F32, tag="c", name="c", bufs=3)
+            c = work.tile([P, JT, U, B], F32, tag="c", name="c", bufs=3)
             c_t[k] = c
-            nc.vector.tensor_tensor(out=c[:], in0=a_t[(k, GF)][:], in1=c0_bc, op=ALU.mult)
+            af = a_t[(k, GF)]
+            nc.vector.tensor_tensor(out=c[:, 0:2, :, :], in0=af[:, 0:2, :, :],
+                                    in1=c0t_p[:, 0:2, :].unsqueeze(2).to_broadcast([P, 2, U, B]), op=ALU.mult)
+            if k == K - 1:
+                nc.vector.tensor_tensor(out=c[:, 2:4, :, :], in0=af[:, 2:4, :, :],
+                                        in1=c0t_p[:, 2:4, :].unsqueeze(2).to_broadcast([P, 2, U, B]), op=ALU.mult)
+            else:
+                nc.gpsimd.tensor_tensor(out=c[:, 2:4, :, :], in0=af[:, 2:4, :, :],
+                                        in1=c0t_sb[:, 2:4, :].unsqueeze(2).to_broadcast([P, 2, U, B]), op=ALU.mult)
 
         def st_b(k):
             ai = a_t[(k, GI)]
             nc.gpsimd.tensor_tensor(out=ai[:], in0=ai[:], in1=a_t[(k, GG)][:], op=ALU.mult)
 
         def st_c(k):
-            eng = nc.vector if k == K - 1 else nc.gpsimd
-            eng.tensor_tensor(out=c_t[k][:], in0=c_t[k][:], in1=a_t[(k, GI)][:], op=ALU.add)
+            for s in range(U):
+                cp = pc.tile([P, H], F32, tag="cp", name="cp")
+                cp_t[(k, s)] = cp
+                for jt in range(JT):
+                    js = slice(jt * P, (jt + 1) * P)
+                    nc.tensor.matmul(cp[:, js], lhsT=c_t[k][:, jt, s, :], rhs=ident_f[:], is_transpose=True,
+                                     start=True, stop=False)
+                    nc.tensor.matmul(cp[:, js], lhsT=a_t[(k, GI)][:, jt, s, :], rhs=ident_f[:], is_transpose=True,
+                                     start=False, stop=True)
 
         def st_tc(k):
             hh = work.tile([P, U, H], F32, tag="hh", name="hh", bufs=4)
             h_t[k] = hh
-            nc.scalar.activation(out=hh[:], in_=c_t[k][:], func=ACT.Tanh)
+            for s in range(U):
+                nc.scalar.activation(out=hh[:, s, :], in_=cp_t[(k, s)][:], func=ACT.Tanh)
+            if k == K - 1:
+                nc.scalar.copy(out=c_last[:], in_=cp_t[(k, U - 1)][:])
 
         def st_x(k):
             eng = nc.vector if k >= K - 2 else nc.gpsimd
@@ -206,55 +269,56 @@ def tile_lstmlayer_kernel(tc, x_in, h0, c0, noise, w_ih, w_hh, b_ih, b_hh, out_h
             nc.sync.dma_start(out=out_h[k * U:(k + 1) * U].rearrange("t b h -> b t h"), in_=hh[:])
             if k == K - 1:
                 nc.sync.dma_start(out=out_state[0], in_=hh[:, U - 1, :])
-                nc.sync.dma_start(out=out_state[1], in_=c_t[k][:, U - 1, :])
+                nc.sync.dma_start(out=out_state[1], in_=c_last[:])
 
         h0_transpose()
         whh_transpose(0)
         x_transpose(0)
+        x_transpose(1)
+        make_g(0)
         wih_transpose(0)
         x_quantise(0)
-        make_g(0)
+        x_quantise(1)
         wih_quantise(0)
-        whh_transpose(1)
-        wih_transpose(1)
+        for cb in range(4):
+            if cb < 3:
+                whh_transpose(cb + 1)
+            else:
+                x_transpose(2)
+            gate_mx(0, cb)
+            if cb < 3:
+                wih_transpose(cb + 1)
+            gate_act(0, cb)
+            if cb == GG:
+                st_b(0)
+            if cb < 3:
+                make_g(cb + 1)
+                wih_quantise(cb + 1)
+            if cb == 0:
+                make_c0t()
+            if cb == 1:
+                make_noise()
+        x_quantise(2)
+        x_transpose(3)
 
-        n_t = 1
-        n_q = 1
-        for it in range(K + 2):
+        for it in range(1, K + 2):
+            if 0 <= it - 2 < K:
+                st_tc(it - 2)
+            if it - 1 < K:
+                st_a(it - 1)
             if 0 <= it - 2 < K:
                 st_x(it - 2)
-            if 0 <= it - 1 < K:
-                st_a(it - 1)
+            if it < K:
+                for cb in range(4):
+                    gate_mx(it, cb)
+                    gate_act(it, cb)
+                    if cb == GG:
+                        st_b(it)
+            if it - 1 < K:
                 st_c(it - 1)
-            if it < K:
-                gate(it, 0)
-                if it == 0:
-                    make_g(1)
-                    wih_quantise(1)
-                    whh_transpose(2)
-                    wih_transpose(2)
-                gate(it, 1)
-                st_b(it)
-                if it == 0:
-                    make_g(2)
-                    wih_quantise(2)
-                    nc.tensor.matmul(c0_p[:], lhsT=ident_b[:], rhs=c0_sb[:], start=True, stop=True)
-                    whh_transpose(3)
-                    wih_transpose(3)
-                gate(it, 2)
-            if 0 <= it - 1 < K:
-                st_tc(it - 1)
-            if it < K:
-                if it == 0:
-                    make_g(3)
-                    wih_quantise(3)
-                    nc.tensor.matmul(noise_p[:], lhsT=ident_b[:], rhs=noise_sb[:], start=True, stop=True)
-                gate(it, 3)
             if 0 <= it - 2 < K:
                 st_h(it - 2)
-            if n_q < n_t:
-                x_quantise(n_q)
-                n_q += 1
-            if n_t < NQ and it < K and (min(it + 3, K - 1) * U + U - 1) // QUAD >= n_t:
-                x_transpose(n_t)
-                n_t += 1
+            if it + 2 < K:
+                x_quantise(it + 2)
+            if it + 3 < K:
+                x_transpose(it + 3)

@@ -227,6 +227,10 @@ def tile_lstmlayer_kernel(tc, x_in, h0, c0, noise, w_ih, w_hh, b_ih, b_hh, out_h
             c = work.tile([P, JT, U, B], F32, tag="c", name="c", bufs=3)
             c_t[k] = c
             af = a_t[(k, GF)]
+            if k % 2 == 0 and k < K - 1:
+                nc.gpsimd.tensor_tensor(out=c[:], in0=af[:],
+                                        in1=c0t_sb[:].unsqueeze(2).to_broadcast([P, JT, U, B]), op=ALU.mult)
+                return
             nc.vector.tensor_tensor(out=c[:, 0:2, :, :], in0=af[:, 0:2, :, :],
                                     in1=c0t_p[:, 0:2, :].unsqueeze(2).to_broadcast([P, 2, U, B]), op=ALU.mult)
             if k == K - 1:

@@ -24,6 +24,7 @@ QUAD = 4
 NQ = T // QUAD
 JT = H // P
 A_BUFS = (4, 3, 3, 5)
+X_GROUPS = ((0,), (1,), (2, 3), (4, 5, 6, 7), (8, 9, 10, 11), (12, 13, 14, 15))
 
 
 def tile_lstmlayer_kernel(tc, x_in, h0, c0, noise, w_ih, w_hh, b_ih, b_hh, out_h, out_state):
@@ -98,21 +99,23 @@ def tile_lstmlayer_kernel(tc, x_in, h0, c0, noise, w_ih, w_hh, b_ih, b_hh, out_h
         w_grp = {}
 
         def x_transpose(m):
+            gq = [g for g in range(len(X_GROUPS)) if m in X_GROUPS[g]][0]
+            pos = X_GROUPS[gq].index(m)
+            if pos == 0:
+                x_grp[gq] = stage.tile([P, len(X_GROUPS[gq]) * U * B * 4], BF16, tag="xgrp", name="xgrp", align_bytes=64)
             rawf = x_raw[m * U // QUAD][:].bitcast(F32)
             s0 = m * U % QUAD
-            grp = stage.tile([P, U * B * 4], BF16, tag="xgrp", name="xgrp", align_bytes=64)
-            x_grp[m] = grp
             pt = ptp.tile([P, 512], F32, tag="tp", name="pt")
             for sl in range(U):
                 for u in range(2):
                     pl = 2 * sl + u
                     nc.tensor.transpose(pt[:, pl * P:(pl + 1) * P], rawf[:, s0 + sl, u * P:(u + 1) * P], ident_f[:])
-            nc.scalar.copy(out=grp[:].bitcast(F32).rearrange("w (s b u) -> w s b u", s=U, u=2),
+            nc.scalar.copy(out=x_grp[gq][:].bitcast(F32)[:, pos * 512:(pos + 1) * 512].rearrange("w (s b u) -> w s b u", s=U, u=2),
                            in_=pt[:].rearrange("w (s u b) -> w s b u", s=U, u=2))
 
-        def x_quantise(m):
-            cols = slice(m * U * B, (m + 1) * U * B)
-            nc.vector.quantize_mx(out=x_codes[:, cols].bitcast(FP8X4), scales=x_scales[:, cols], in_=x_grp[m][:])
+        def x_quantise(gq):
+            cols = slice(X_GROUPS[gq][0] * U * B, (X_GROUPS[gq][-1] + 1) * U * B)
+            nc.vector.quantize_mx(out=x_codes[:, cols].bitcast(FP8X4), scales=x_scales[:, cols], in_=x_grp[gq][:])
 
         def h0_transpose():
             pt = ptp.tile([P, 512], F32, tag="tp", name="pth0")
@@ -227,10 +230,6 @@ def tile_lstmlayer_kernel(tc, x_in, h0, c0, noise, w_ih, w_hh, b_ih, b_hh, out_h
             c = work.tile([P, JT, U, B], F32, tag="c", name="c", bufs=3)
             c_t[k] = c
             af = a_t[(k, GF)]
-            if k % 2 == 0 and k < K - 1:
-                nc.gpsimd.tensor_tensor(out=c[:], in0=af[:],
-                                        in1=c0t_sb[:].unsqueeze(2).to_broadcast([P, JT, U, B]), op=ALU.mult)
-                return
             nc.vector.tensor_tensor(out=c[:, 0:2, :, :], in0=af[:, 0:2, :, :],
                                     in1=c0t_p[:, 0:2, :].unsqueeze(2).to_broadcast([P, 2, U, B]), op=ALU.mult)
             if k == K - 1:
@@ -287,8 +286,8 @@ def tile_lstmlayer_kernel(tc, x_in, h0, c0, noise, w_ih, w_hh, b_ih, b_hh, out_h
         for cb in range(4):
             if cb < 3:
                 whh_transpose(cb + 1)
-            else:
-                x_transpose(2)
+            if cb >= 2:
+                x_transpose(cb)
             gate_mx(0, cb)
             if cb < 3:
                 wih_transpose(cb + 1)
@@ -303,7 +302,7 @@ def tile_lstmlayer_kernel(tc, x_in, h0, c0, noise, w_ih, w_hh, b_ih, b_hh, out_h
             if cb == 1:
                 make_noise()
         x_quantise(2)
-        x_transpose(3)
+        x_transpose(4)
 
         for it in range(1, K + 2):
             if 0 <= it - 2 < K:
@@ -318,11 +317,13 @@ def tile_lstmlayer_kernel(tc, x_in, h0, c0, noise, w_ih, w_hh, b_ih, b_hh, out_h
                     gate_act(it, cb)
                     if cb == GG:
                         st_b(it)
+                        if 2 * it + 3 < K:
+                            x_transpose(2 * it + 3)
             if it - 1 < K:
                 st_c(it - 1)
             if 0 <= it - 2 < K:
                 st_h(it - 2)
-            if it + 2 < K:
-                x_quantise(it + 2)
-            if it + 3 < K:
-                x_transpose(it + 3)
+            if it in (2, 4, 6):
+                x_quantise(it // 2 + 2)
+            if 2 * it + 4 < K:
+                x_transpose(2 * it + 4)

@@ -315,6 +315,8 @@ def tile_lstmlayer_kernel(tc, x_in, h0, c0, noise, w_ih, w_hh, b_ih, b_hh, out_h
                 for cb in range(4):
                     gate_mx(it, cb)
                     gate_act(it, cb)
+                    if cb == GI and it in (3, 5, 7):
+                        x_quantise(it // 2 + 2)
                     if cb == GG:
                         st_b(it)
                         if 2 * it + 3 < K:
@@ -323,7 +325,5 @@ def tile_lstmlayer_kernel(tc, x_in, h0, c0, noise, w_ih, w_hh, b_ih, b_hh, out_h
                 st_c(it - 1)
             if 0 <= it - 2 < K:
                 st_h(it - 2)
-            if it in (2, 4, 6):
-                x_quantise(it // 2 + 2)
             if 2 * it + 4 < K:
                 x_transpose(2 * it + 4)

@@ -82,10 +82,13 @@ def tile_lstmlayer_kernel(tc, x_in, h0, c0, noise, w_ih, w_hh, b_ih, b_hh, out_h
 
         nc.sync.dma_start(out=h0_sb[:], in_=h0)
         whh_raw = [load_w(w_hh, 0)]
-        x_raw = [load_x(0)]
         wih_raw = [load_w(w_ih, 0)]
+        x_first = raws.tile([P, QUAD, I], BF16, tag="raw", name="xraw")
+        x_raw = [x_first]
+        nc.sync.dma_start(out=x_first[:, 0:U, :], in_=x_in[0:U].rearrange("t b k -> b t k"))
         nc.sync.dma_start(out=bias_rows[0:1, :], in_=b_ih.rearrange("(o n) -> o n", o=1))
         nc.sync.dma_start(out=bias_rows[1:2, :], in_=b_hh.rearrange("(o n) -> o n", o=1))
+        nc.sync.dma_start(out=x_first[:, U:QUAD, :], in_=x_in[U:QUAD].rearrange("t b k -> b t k"))
         for cb in range(1, 4):
             whh_raw.append(load_w(w_hh, cb))
             wih_raw.append(load_w(w_ih, cb))
@@ -261,34 +264,42 @@ def tile_lstmlayer_kernel(tc, x_in, h0, c0, noise, w_ih, w_hh, b_ih, b_hh, out_h
                 nc.scalar.activation(out=hh[:, s, :], in_=cp_t[(k, s)][:], func=ACT.Tanh)
             if k == K - 1:
                 nc.scalar.copy(out=c_last[:], in_=cp_t[(k, U - 1)][:])
+                nc.sync.dma_start(out=out_state[1], in_=c_last[:])
 
         def st_x(k):
+            if k == K - 1:
+                return
             eng = nc.vector if k >= K - 2 else nc.gpsimd
             eng.tensor_tensor(out=h_t[k][:], in0=h_t[k][:], in1=a_t[(k, GO)][:], op=ALU.mult)
 
         def st_h(k):
             hh = h_t[k]
+            if k == K - 1:
+                for s in range(U):
+                    nc.vector.tensor_tensor(out=hh[:, s, :], in0=hh[:, s, :], in1=a_t[(k, GO)][:, s, :], op=ALU.mult)
+                    nc.vector.tensor_tensor(out=hh[:, s, :], in0=hh[:, s, :], in1=cn_p[:, 1, :], op=ALU.add)
+                    nc.sync.dma_start(out=out_h[k * U + s], in_=hh[:, s, :])
+                nc.sync.dma_start(out=out_state[0], in_=hh[:, U - 1, :])
+                return
             nc.vector.tensor_tensor(out=hh[:], in0=hh[:], in1=noise_bc, op=ALU.add)
             nc.sync.dma_start(out=out_h[k * U:(k + 1) * U].rearrange("t b h -> b t h"), in_=hh[:])
-            if k == K - 1:
-                nc.sync.dma_start(out=out_state[0], in_=hh[:, U - 1, :])
-                nc.sync.dma_start(out=out_state[1], in_=c_last[:])
 
         h0_transpose()
         whh_transpose(0)
-        x_transpose(0)
-        x_transpose(1)
-        make_g(0)
         wih_transpose(0)
-        x_quantise(0)
-        x_quantise(1)
+        make_g(0)
+        x_transpose(0)
         wih_quantise(0)
+        x_quantise(0)
+        x_transpose(1)
         for cb in range(4):
             if cb < 3:
                 whh_transpose(cb + 1)
             if cb >= 2:
                 x_transpose(cb)
             gate_mx(0, cb)
+            if cb == 0:
+                x_quantise(1)
             if cb < 3:
                 wih_transpose(cb + 1)
             gate_act(0, cb)
@@ -297,10 +308,8 @@ def tile_lstmlayer_kernel(tc, x_in, h0, c0, noise, w_ih, w_hh, b_ih, b_hh, out_h
             if cb < 3:
                 make_g(cb + 1)
                 wih_quantise(cb + 1)
-            if cb == 0:
-                make_c0t()
-            if cb == 1:
-                make_noise()
+        make_c0t()
+        make_noise()
         x_quantise(2)
         x_transpose(4)
 

from contextlib import ExitStack

import concourse.mybir as mybir
from concourse.masks import make_identity

F32 = mybir.dt.float32
BF16 = mybir.dt.bfloat16
U32 = mybir.dt.uint32
U8 = mybir.dt.uint8
FP8X4 = mybir.dt.float8_e4m3fn_x4
ACT = mybir.ActivationFunctionType
ALU = mybir.AluOpType

T, B, I, H = 32, 128, 512, 512
P = 128
FLOPS = 2 * T * B * I * 4 * H + 2 * B * H * 4 * H

GI, GG, GF, GO = 0, 1, 2, 3
GATE_ROW0 = (0, 1024, 512, 1536)
GATE_FUNC = (ACT.Sigmoid, ACT.Tanh, ACT.Sigmoid, ACT.Sigmoid)
U = 2
K = T // U
QUAD = 4
NQ = T // QUAD
JT = H // P
A_BUFS = (4, 3, 3, 5)
X_GROUPS = ((0,), (1,), (2, 3), (4, 5, 6, 7), (8, 9, 10, 11), (12, 13, 14, 15))


def tile_lstmlayer_kernel(tc, x_in, h0, c0, noise, w_ih, w_hh, b_ih, b_hh, out_h, out_state):
    nc = tc.nc
    with ExitStack() as ctx:
        const = ctx.enter_context(tc.tile_pool(name="const", bufs=1))
        raws = ctx.enter_context(tc.tile_pool(name="raws", bufs=12))
        stage = ctx.enter_context(tc.tile_pool(name="stage", bufs=2))
        work = ctx.enter_context(tc.tile_pool(name="work", bufs=3))
        pconst = ctx.enter_context(tc.psum_pool(name="pconst", bufs=1))
        pz = ctx.enter_context(tc.psum_pool(name="pz", bufs=4))
        pc = ctx.enter_context(tc.psum_pool(name="pc", bufs=2))
        ptp = ctx.enter_context(tc.psum_pool(name="ptp", bufs=1))
        ctx.enter_context(tc.manual_schedule())

        ident_f = const.tile([P, P], F32, name="ident_f")
        make_identity(nc, ident_f[:])
        ident_b = const.tile([P, P], BF16, name="ident_b")
        make_identity(nc, ident_b[:])
        ones_b = const.tile([P, P], BF16, name="ones_b")
        nc.vector.memset(ones_b[:], 1.0)
        bias_rows = const.tile([P, 4 * H], BF16, name="bias_rows")
        nc.vector.memset(bias_rows[:], 0.0)
        warm = const.tile([P, 1], F32, name="warm")
        nc.vector.memset(warm[:], 0.0)
        warm2 = const.tile([P, 1], F32, name="warm2")
        nc.scalar.activation(out=warm2[:], in_=warm[:], func=ACT.Sigmoid)

        g_t = const.tile([P, 3, JT, B], F32, name="g_t")
        g_o = const.tile([P, H], F32, name="g_o")
        w_codes = const.tile([P, 4 * H], U32, name="w_codes", align_bytes=64)
        w_scales = const.tile([P, 4 * H], U8, name="w_scales", align_bytes=64)
        x_codes = const.tile([P, T * B], U32, name="x_codes", align_bytes=64)
        x_scales = const.tile([P, T * B], U8, name="x_scales", align_bytes=64)
        whh_t = const.tile([P, 2, 4 * H], F32, name="whh_t")
        h0_t = const.tile([P, 2, B], F32, name="h0_t")
        h0_sb = const.tile([P, H], BF16, name="h0_sb")
        c0_sb = const.tile([P, H], BF16, name="c0_sb")
        noise_sb = const.tile([P, H], BF16, name="noise_sb")
        c0t_sb = const.tile([P, JT, B], F32, name="c0t_sb")
        c_last = const.tile([P, H], F32, name="c_last")
        whh_b = whh_t[:].bitcast(BF16).rearrange("w u (j e) -> w u j e", e=2)
        h0_b = h0_t[:].bitcast(BF16).rearrange("w u (b e) -> w u b e", e=2)

        def load_x(q):
            raw = raws.tile([P, QUAD, I], BF16, tag="raw", name="xraw")
            nc.sync.dma_start(out=raw[:], in_=x_in[QUAD * q:QUAD * (q + 1)].rearrange("t b k -> b t k"))
            return raw

        def load_w(w, cb):
            r0 = GATE_ROW0[cb]
            raw = raws.tile([P, 4, I], BF16, tag="raw", name="wraw")
            nc.sync.dma_start(out=raw[:], in_=w[r0:r0 + 512, :].rearrange("(p a) k -> p a k", a=4))
            return raw

        nc.sync.dma_start(out=h0_sb[:], in_=h0)
        whh_raw = [load_w(w_hh, 0)]
        wih_raw = [load_w(w_ih, 0)]
        x_first = raws.tile([P, QUAD, I], BF16, tag="raw", name="xraw")
        x_raw = [x_first]
        nc.sync.dma_start(out=x_first[:, 0:U, :], in_=x_in[0:U].rearrange("t b k -> b t k"))
        nc.sync.dma_start(out=bias_rows[0:1, :], in_=b_ih.rearrange("(o n) -> o n", o=1))
        nc.sync.dma_start(out=bias_rows[1:2, :], in_=b_hh.rearrange("(o n) -> o n", o=1))
        nc.sync.dma_start(out=x_first[:, U:QUAD, :], in_=x_in[U:QUAD].rearrange("t b k -> b t k"))
        for cb in range(1, 4):
            whh_raw.append(load_w(w_hh, cb))
            wih_raw.append(load_w(w_ih, cb))
            if cb == 1:
                nc.sync.dma_start(out=c0_sb[:], in_=c0)
                nc.sync.dma_start(out=noise_sb[:], in_=noise)
        for q in range(1, NQ):
            x_raw.append(load_x(q))

        x_grp = {}
        w_grp = {}

        def x_transpose(m):
            gq = [g for g in range(len(X_GROUPS)) if m in X_GROUPS[g]][0]
            pos = X_GROUPS[gq].index(m)
            if pos == 0:
                x_grp[gq] = stage.tile([P, len(X_GROUPS[gq]) * U * B * 4], BF16, tag="xgrp", name="xgrp", align_bytes=64)
            rawf = x_raw[m * U // QUAD][:].bitcast(F32)
            s0 = m * U % QUAD
            pt = ptp.tile([P, 512], F32, tag="tp", name="pt")
            for sl in range(U):
                for u in range(2):
                    pl = 2 * sl + u
                    nc.tensor.transpose(pt[:, pl * P:(pl + 1) * P], rawf[:, s0 + sl, u * P:(u + 1) * P], ident_f[:])
            nc.scalar.copy(out=x_grp[gq][:].bitcast(F32)[:, pos * 512:(pos + 1) * 512].rearrange("w (s b u) -> w s b u", s=U, u=2),
                           in_=pt[:].rearrange("w (s u b) -> w s b u", s=U, u=2))

        def x_quantise(gq):
            cols = slice(X_GROUPS[gq][0] * U * B, (X_GROUPS[gq][-1] + 1) * U * B)
            nc.vector.quantize_mx(out=x_codes[:, cols].bitcast(FP8X4), scales=x_scales[:, cols], in_=x_grp[gq][:])

        def h0_transpose():
            pt = ptp.tile([P, 512], F32, tag="tp", name="pth0")
            h0f = h0_sb[:].bitcast(F32)
            for u in range(2):
                nc.tensor.transpose(pt[:, u * P:(u + 1) * P], h0f[:, u * P:(u + 1) * P], ident_f[:])
            nc.vector.tensor_copy(out=h0_t[:].rearrange("w u b -> w (u b)"), in_=pt[:, 0:2 * P])

        def wih_transpose(cb):
            rawf = wih_raw[cb][:].bitcast(F32)
            grp = stage.tile([P, 512 * 4], BF16, tag="wgrp", name="wgrp", align_bytes=64)
            w_grp[cb] = grp
            grpf = grp[:].bitcast(F32).rearrange("w (p a u) -> w p a u", a=4, u=2)
            for half in range(2):
                pt = pz.tile([P, 512], F32, tag="z", name="ptw")
                for al in range(2):
                    for u in range(2):
                        pl = 2 * al + u
                        nc.tensor.transpose(pt[:, pl * P:(pl + 1) * P], rawf[:, 2 * half + al, u * P:(u + 1) * P], ident_f[:])
                nc.vector.tensor_copy(out=grpf[:, :, 2 * half:2 * half + 2, :],
                                      in_=pt[:].rearrange("w (a u p) -> w p a u", a=2, u=2))

        def wih_quantise(cb):
            cols = slice(cb * 512, (cb + 1) * 512)
            nc.vector.quantize_mx(out=w_codes[:, cols].bitcast(FP8X4), scales=w_scales[:, cols], in_=w_grp[cb][:])

        def whh_transpose(cb):
            rawf = whh_raw[cb][:].bitcast(F32)
            for u in range(2):
                pt = pz.tile([P, 512], F32, tag="z", name="pth")
                for a in range(4):
                    nc.tensor.transpose(pt[:, a * P:(a + 1) * P], rawf[:, a, u * P:(u + 1) * P], ident_f[:])
                nc.scalar.copy(out=whh_t[:, u, cb * 512:(cb + 1) * 512].rearrange("w (p a) -> w p a", a=4),
                               in_=pt[:].rearrange("w (a p) -> w p a", a=4))

        def make_g(cb):
            r0 = GATE_ROW0[cb]
            zt = pz.tile([P, 512], F32, tag="z", name="zg")
            if cb == GO:
                cols = slice(cb * 512, (cb + 1) * 512)
                nc.tensor.matmul(zt[:], lhsT=ones_b[:], rhs=bias_rows[:, r0:r0 + 512], start=True, stop=False)
                for u in range(2):
                    for e in range(2):
                        nc.tensor.matmul(zt[:], lhsT=h0_b[:, u, :, e], rhs=whh_b[:, u, cols, e],
                                         start=False, stop=(u == 1 and e == 1))
                nc.scalar.copy(out=g_o[:], in_=zt[:])
            else:
                for jt in range(JT):
                    js = slice(jt * P, (jt + 1) * P)
                    nc.tensor.matmul(zt[:, js], lhsT=bias_rows[:, r0 + jt * P:r0 + (jt + 1) * P], rhs=ones_b[:],
                                     start=True, stop=False)
                    for u in range(2):
                        for e in range(2):
                            nc.tensor.matmul(zt[:, js], lhsT=whh_b[:, u, cb * 512 + jt * P:cb * 512 + (jt + 1) * P, e],
                                             rhs=h0_b[:, u, :, e], start=False, stop=(u == 1 and e == 1))
                nc.scalar.copy(out=g_t[:, cb, :, :].rearrange("p j b -> p (j b)"), in_=zt[:])

        cn_p = pconst.tile([P, 2, H], BF16, name="cn_p")

        def make_c0t():
            for jt in range(JT):
                js = slice(jt * P, (jt + 1) * P)
                nc.tensor.matmul(cn_p[:, 0, js], lhsT=c0_sb[:, js], rhs=ident_b[:], start=True, stop=True)
            nc.vector.tensor_copy(out=c0t_sb[:].rearrange("p j b -> p (j b)"), in_=cn_p[:, 0, :])

        def make_noise():
            nc.tensor.matmul(cn_p[:, 1, :], lhsT=ident_b[:], rhs=noise_sb[:], start=True, stop=True)

        c0t_p = cn_p[:, 0, :].rearrange("p (j b) -> p j b", j=JT)
        noise_bc = cn_p[:, 1, :].unsqueeze(1).to_broadcast([P, U, H])

        a_t = {}
        c_t = {}
        cp_t = {}
        h_t = {}

        def gate_mx(k, cb):
            xc = slice(k * U * B, (k + 1) * U * B)
            if cb == GO:
                a = work.tile([P, U, H], F32, tag="a3", name="a3", bufs=A_BUFS[cb])
                cols = slice(cb * 512, (cb + 1) * 512)
                for s in range(U):
                    t = k * U + s
                    xs = slice(t * B, (t + 1) * B)
                    z = pz.tile([P, 512], F32, tag="z", name="z")
                    nc.tensor.matmul_mx(z[:], lhsT=x_codes[:, xs].bitcast(FP8X4), lhsT_scale=x_scales[:, xs],
                                        rhs=w_codes[:, cols].bitcast(FP8X4), rhs_scale=w_scales[:, cols],
                                        start=True, stop=True)
                    nc.vector.tensor_tensor(out=a[:, s, :], in0=z[:], in1=g_o[:], op=ALU.add)
            else:
                a = work.tile([P, JT, U, B], F32, tag="a%d" % cb, name="a%d" % cb, bufs=A_BUFS[cb])
                for bk in range(2):
                    z = pz.tile([P, 512], F32, tag="z", name="z")
                    for jl in range(2):
                        jt = 2 * bk + jl
                        wc = slice(cb * 512 + jt * P, cb * 512 + (jt + 1) * P)
                        nc.tensor.matmul_mx(z[:, jl * U * B:(jl + 1) * U * B],
                                            lhsT=w_codes[:, wc].bitcast(FP8X4), lhsT_scale=w_scales[:, wc],
                                            rhs=x_codes[:, xc].bitcast(FP8X4), rhs_scale=x_scales[:, xc],
                                            start=True, stop=True)
                    nc.vector.tensor_tensor(out=a[:, 2 * bk:2 * bk + 2, :, :],
                                            in0=z[:].rearrange("p (j t b) -> p j t b", j=2, t=U),
                                            in1=g_t[:, cb, 2 * bk:2 * bk + 2, :].unsqueeze(2).to_broadcast([P, 2, U, B]),
                                            op=ALU.add)
            a_t[(k, cb)] = a

        def gate_act(k, cb):
            a = a_t[(k, cb)]
            nc.scalar.activation(out=a[:], in_=a[:], func=GATE_FUNC[cb])

        def st_a(k):
            c = work.tile([P, JT, U, B], F32, tag="c", name="c", bufs=3)
            c_t[k] = c
            af = a_t[(k, GF)]
            nc.vector.tensor_tensor(out=c[:, 0:2, :, :], in0=af[:, 0:2, :, :],
                                    in1=c0t_p[:, 0:2, :].unsqueeze(2).to_broadcast([P, 2, U, B]), op=ALU.mult)
            if k == K - 1:
                nc.vector.tensor_tensor(out=c[:, 2:4, :, :], in0=af[:, 2:4, :, :],
                                        in1=c0t_p[:, 2:4, :].unsqueeze(2).to_broadcast([P, 2, U, B]), op=ALU.mult)
            else:
                nc.gpsimd.tensor_tensor(out=c[:, 2:4, :, :], in0=af[:, 2:4, :, :],
                                        in1=c0t_sb[:, 2:4, :].unsqueeze(2).to_broadcast([P, 2, U, B]), op=ALU.mult)

        def st_b(k):
            ai = a_t[(k, GI)]
            nc.gpsimd.tensor_tensor(out=ai[:], in0=ai[:], in1=a_t[(k, GG)][:], op=ALU.mult)

        def st_c(k):
            for s in range(U):
                cp = pc.tile([P, H], F32, tag="cp", name="cp")
                cp_t[(k, s)] = cp
                for jt in range(JT):
                    js = slice(jt * P, (jt + 1) * P)
                    nc.tensor.matmul(cp[:, js], lhsT=c_t[k][:, jt, s, :], rhs=ident_f[:], is_transpose=True,
                                     start=True, stop=False)
                    nc.tensor.matmul(cp[:, js], lhsT=a_t[(k, GI)][:, jt, s, :], rhs=ident_f[:], is_transpose=True,
                                     start=False, stop=True)

        def st_tc(k):
            hh = work.tile([P, U, H], F32, tag="hh", name="hh", bufs=4)
            h_t[k] = hh
            for s in range(U):
                nc.scalar.activation(out=hh[:, s, :], in_=cp_t[(k, s)][:], func=ACT.Tanh)
            if k == K - 1:
                nc.scalar.copy(out=c_last[:], in_=cp_t[(k, U - 1)][:])
                nc.sync.dma_start(out=out_state[1], in_=c_last[:])

        def st_x(k):
            if k == K - 1:
                return
            eng = nc.vector if k >= K - 2 else nc.gpsimd
            eng.tensor_tensor(out=h_t[k][:], in0=h_t[k][:], in1=a_t[(k, GO)][:], op=ALU.mult)

        def st_h(k):
            hh = h_t[k]
            if k == K - 1:
                for s in range(U):
                    nc.vector.tensor_tensor(out=hh[:, s, :], in0=hh[:, s, :], in1=a_t[(k, GO)][:, s, :], op=ALU.mult)
                    nc.vector.tensor_tensor(out=hh[:, s, :], in0=hh[:, s, :], in1=cn_p[:, 1, :], op=ALU.add)
                    nc.sync.dma_start(out=out_h[k * U + s], in_=hh[:, s, :])
                nc.sync.dma_start(out=out_state[0], in_=hh[:, U - 1, :])
                return
            nc.vector.tensor_tensor(out=hh[:], in0=hh[:], in1=noise_bc, op=ALU.add)
            nc.sync.dma_start(out=out_h[k * U:(k + 1) * U].rearrange("t b h -> b t h"), in_=hh[:])

        h0_transpose()
        whh_transpose(0)
        wih_transpose(0)
        make_g(0)
        x_transpose(0)
        wih_quantise(0)
        x_quantise(0)
        x_transpose(1)
        for cb in range(4):
            if cb < 3:
                whh_transpose(cb + 1)
            if cb >= 2:
                x_transpose(cb)
            gate_mx(0, cb)
            if cb == 0:
                x_quantise(1)
            if cb < 3:
                wih_transpose(cb + 1)
            gate_act(0, cb)
            if cb == GG:
                st_b(0)
            if cb < 3:
                make_g(cb + 1)
                wih_quantise(cb + 1)
        make_c0t()
        make_noise()
        x_quantise(2)
        x_transpose(4)

        for it in range(1, K + 2):
            if 0 <= it - 2 < K:
                st_tc(it - 2)
            if it - 1 < K:
                st_a(it - 1)
            if 0 <= it - 2 < K:
                st_x(it - 2)
            if it < K:
                for cb in range(4):
                    gate_mx(it, cb)
                    gate_act(it, cb)
                    if cb == GI and it in (3, 5, 7):
                        x_quantise(it // 2 + 2)
                    if cb == GG:
                        st_b(it)
                        if 2 * it + 3 < K:
                            x_transpose(2 * it + 3)
            if it - 1 < K:
                st_c(it - 1)
            if 0 <= it - 2 < K:
                st_h(it - 2)
            if 2 * it + 4 < K:
                x_transpose(2 * it + 4)
